import numpy as np
import ml_dtypes


def mxq(x, axis, fmt="e4m3"):
    dtype, down = {"e4m3": (ml_dtypes.float8_e4m3fn, 7), "e5m2": (ml_dtypes.float8_e5m2, 14)}[fmt]
    v = np.moveaxis(np.asarray(x, np.float32).astype(ml_dtypes.bfloat16).astype(np.float64), axis, -1)
    blocks = v.reshape(v.shape[:-1] + (-1, 32))
    amax = np.abs(blocks).max(-1, keepdims=True)
    byte = np.maximum(np.where(amax > 0, np.frexp(amax)[1] - 1 + 127, 0) - down, 1)
    scale = np.exp2(byte - 127.0)
    codes = (blocks / scale).astype(np.float32).astype(dtype).astype(np.float64)
    return np.moveaxis((codes * scale).reshape(v.shape), -1, axis)


WIDE = False


def mx_kscale(k):
    if not WIDE:
        return np.ones(k)
    levels = np.array([10, -10, 5, -5, 0])
    a = np.random.permutation(np.resize(levels, k // 512 * 4)).reshape(k // 512, 4)
    idx = np.arange(k)
    return np.exp2(a[idx // 512, idx % 128 // 32])


BF16 = ml_dtypes.bfloat16


def bf(x):
    return np.asarray(x, np.float32).astype(BF16)


def f64(x):
    return np.asarray(x).astype(np.float64)


NK, B, C, HP, CIN = 2, 16, 1024, 8, 256
H = 2 * HP
E = 0.01
BN_EPS = 1e-5


def _stab(z, e):
    return z + np.where(z >= 0, e, -e)


def away(shape):
    z = np.random.standard_normal(shape)
    return np.sign(z) * (0.05 + 0.2 * np.abs(z))


def setup_inputs():
    s = mx_kscale(C)
    return {
        "rK_stack": bf(np.random.standard_normal((NK, B, C, HP, HP)) * 0.2 / np.sqrt(NK)),
        "aK_stack": bf(away((NK, B, C, HP, HP))),
        "gamma": bf(np.random.uniform(0.5, 1.5, (NK, C)) * 0.01 * s),
        "var": bf(np.random.uniform(0.5, 1.5, (NK, C)) * 1e-4),
        "aKPool": bf(away((B, C, HP, HP))),
        "aJ_pool": bf(np.random.uniform(0.0, 1.0, (B, C, H, H))),
        "aK_conv": bf(away((B, C, H, H))),
        "aJ_conv": bf(np.random.uniform(0.0, 1.0, (B, CIN, H, H))),
        "W_conv": bf(np.random.standard_normal((C, CIN)) / np.sqrt(C) / s[:, None]),
    }


def reference(rK_stack, aK_stack, gamma, var, aKPool, aJ_pool, aK_conv, aJ_conv, W_conv):
    w = f64(gamma) * (1.0 / np.sqrt(f64(var) + BN_EPS))
    s = (f64(rK_stack) / _stab(f64(aK_stack), E)) * w[:, None, :, None, None]
    s_total = np.sum(s, axis=0)
    a_pool = f64(aKPool)
    r_pool = a_pool * s_total
    s_pool = r_pool / _stab(a_pool, E)
    c = np.repeat(np.repeat(s_pool, 2, axis=-2), 2, axis=-1) * 0.25
    R = f64(aJ_pool) * c
    sc = R / _stab(f64(aK_conv), E)
    cJ = (mxq(f64(W_conv), 0, "e4m3").T @ mxq(sc.reshape(B, C, H * H), 1, "e4m3")).reshape(B, CIN, H, H)
    return f64(aJ_conv) * cJ

@@ -1,0 +1,242 @@
+from contextlib import ExitStack
+
+import concourse.mybir as mybir
+
+FP8X4 = mybir.dt.float8_e4m3fn_x4
+BF16 = mybir.dt.bfloat16
+F32 = mybir.dt.float32
+I32 = mybir.dt.int32
+U32 = mybir.dt.uint32
+U8 = mybir.dt.uint8
+ALU = mybir.AluOpType
+ACT = mybir.ActivationFunctionType
+
+P = 128
+NK = 2
+B = 16
+G = 2
+J = 4
+HW = 256
+CELL = 64
+OT = 2
+CB = 2
+NCH = B // CB
+E = 0.01
+BN_EPS = 1e-5
+SIGN_SCALE = 2.0 ** 64
+SIGN_BIAS = 1e-25
+ABS_MASK = 0x7FFF7FFF
+SIGN_K_ON_S = True
+KAPPA = 0.5 if SIGN_K_ON_S else 1.0
+
+FLOPS = 2 * B * HW * 1024 * 256
+
+
+def tile_lrpdensenettransition_t_kernel(
+    tc, rK_stack, aK_stack, gamma, var, aKPool, aJ_pool, aK_conv, aJ_conv, W_conv, out
+):
+    nc = tc.nc
+    NP = CB * G * J * CELL
+    NS = NK * NP
+    NB = G * J * HW
+    NZ = CB * NB
+    NW = NK * G * J
+
+    rK_v = rK_stack.rearrange("n b (g p j) h w -> p n (b g) (j h w)", g=G, p=P, j=J)
+    aK_v = aK_stack.rearrange("n b (g p j) h w -> p n (b g) (j h w)", g=G, p=P, j=J)
+    aP_v = aKPool.rearrange("b (g p j) h w -> p (b g) (j h w)", g=G, p=P, j=J)
+    a_v = aJ_pool.rearrange("b (g p j) h w -> p (b g) (j h w)", g=G, p=P, j=J)
+    z_v = aK_conv.rearrange("b (g p j) h w -> p (b g) (j h w)", g=G, p=P, j=J)
+    aJ_v = aJ_conv.rearrange("b (t p) h w -> p (b t) (h w)", t=OT, p=P)
+    out_v = out.rearrange("b (t p) h w -> p (b t) (h w)", t=OT, p=P)
+
+    with ExitStack() as ctx:
+        const = ctx.enter_context(tc.tile_pool(name="const", bufs=1))
+        pin = ctx.enter_context(tc.tile_pool(name="pin", bufs=2))
+        one = ctx.enter_context(tc.tile_pool(name="one", bufs=1))
+        two = ctx.enter_context(tc.tile_pool(name="two", bufs=2))
+        ajp = ctx.enter_context(tc.tile_pool(name="ajp", bufs=4))
+        outp = ctx.enter_context(tc.tile_pool(name="outp", bufs=3))
+        psum = ctx.enter_context(tc.psum_pool(name="psum", bufs=2))
+        ctx.enter_context(tc.manual_schedule())
+
+        gam = const.tile([P, NW], BF16, name="gam")
+        vr = const.tile([P, NW], BF16, name="vr")
+        rs = const.tile([P, NW], F32, name="rs")
+        w_t = const.tile([P, NW], F32, name="w_t")
+        w_raw = const.tile([P, G, J, 256], BF16, name="w_raw")
+        w_grp = const.tile([P, G, 256, J], BF16, name="w_grp", align_bytes=64)
+        w_codes = const.tile([P, G * 256], U32, name="w_codes", align_bytes=64)
+        w_scl = const.tile([P, G * 256], U8, name="w_scl", align_bytes=64)
+        T = {}
+
+        def rows(ap, r):
+            return ap.rearrange("p (a r) -> p a r", r=r)
+
+        def load(c):
+            b0 = c * CB
+            sl = slice(G * b0, G * (b0 + CB))
+            for nm, n_cols in (("aK", NS), ("aP", NP), ("z", NZ), ("rK", NS), ("a", NZ)):
+                T[nm, c] = pin.tile([P, n_cols], BF16, name=nm + "_t")
+            T["aJ", c] = ajp.tile([P, CB * OT * HW], BF16, name="aJ_t")
+            for n in range(NK):
+                nc.sync.dma_start(out=rows(T["aK", c][:, n * NP:(n + 1) * NP], J * CELL), in_=aK_v[:, n, sl, :])
+            nc.sync.dma_start(out=rows(T["z", c][:], J * HW), in_=z_v[:, sl, :])
+            nc.sync.dma_start(out=rows(T["aP", c][:], J * CELL), in_=aP_v[:, sl, :])
+            for n in range(NK):
+                nc.sync.dma_start(out=rows(T["rK", c][:, n * NP:(n + 1) * NP], J * CELL), in_=rK_v[:, n, sl, :])
+            nc.sync.dma_start(out=rows(T["a", c][:], J * HW), in_=a_v[:, sl, :])
+            nc.sync.dma_start(out=rows(T["aJ", c][:], HW), in_=aJ_v[:, OT * b0:OT * (b0 + CB), :])
+
+        def v_abs(dst, src):
+            nc.vector.tensor_scalar(
+                out=dst[:].bitcast(I32), in0=src[:].bitcast(I32),
+                scalar1=ABS_MASK, scalar2=None, op0=ALU.bitwise_and,
+            )
+
+        def v_half_sign(dst, src):
+            nc.vector.tensor_scalar(out=dst[:], in0=src[:], scalar1=0.0, scalar2=0.5, op0=ALU.is_ge, op1=ALU.subtract)
+
+        def s_sign(c):
+            if SIGN_K_ON_S:
+                T["sgK", c] = one.tile([P, NS], BF16, name="sgK")
+                nc.scalar.activation(out=T["sgK", c][:], in_=T["aK", c][:], func=ACT.Sign, bias=SIGN_BIAS, scale=SIGN_SCALE)
+
+        def early_a(c):
+            T["absK", c] = one.tile([P, NS], BF16, name="absK")
+            T["absZ", c] = one.tile([P, NZ], BF16, name="absZ")
+            T["absP", c] = two.tile([P, NP], BF16, name="absP")
+            v_abs(T["absK", c], T["aK", c])
+            v_abs(T["absZ", c], T["z", c])
+            v_abs(T["absP", c], T["aP", c])
+
+        def early_b(c):
+            if not SIGN_K_ON_S:
+                T["sgK", c] = one.tile([P, NS], BF16, name="sgK")
+                v_half_sign(T["sgK", c], T["aK", c])
+            T["rKs", c] = one.tile([P, NS], BF16, name="rKs")
+            nc.vector.tensor_tensor(out=T["rKs", c][:], in0=T["rK", c][:], in1=T["sgK", c][:], op=ALU.mult)
+            hZ = one.tile([P, NZ], BF16, name="hZ")
+            v_half_sign(hZ, T["z", c])
+            T["as", c] = one.tile([P, NZ], BF16, name="as_t")
+            nc.vector.tensor_tensor(out=T["as", c][:], in0=T["a", c][:], in1=hZ[:], op=ALU.mult)
+
+        def s_ln(c):
+            T["LK", c] = two.tile([P, NS], F32, name="LK")
+            T["LZ", c] = two.tile([P, NZ], F32, name="LZ")
+            T["LP", c] = two.tile([P, NP], F32, name="LP")
+            nc.scalar.activation(out=T["LK", c][:], in_=T["absK", c][:], func=ACT.Ln, bias=E, scale=1.0)
+            nc.scalar.activation(out=T["LZ", c][:], in_=T["absZ", c][:], func=ACT.Ln, bias=E, scale=1.0)
+            nc.scalar.activation(out=T["LP", c][:], in_=T["absP", c][:], func=ACT.Ln, bias=E, scale=1.0)
+            if c == 0:
+                nc.scalar.activation(out=rs[:], in_=vr[:], func=ACT.Ln, bias=BN_EPS, scale=1.0)
+
+        def s_exp(c):
+            if c == 0:
+                nc.scalar.activation(out=rs[:], in_=rs[:], func=ACT.Exp, scale=-0.5)
+            nc.scalar.activation(out=T["LK", c][:], in_=T["LK", c][:], func=ACT.Exp, scale=-1.0)
+            nc.scalar.activation(out=T["LP", c][:], in_=T["LP", c][:], func=ACT.Exp, scale=-1.0)
+            for bl in range(CB):
+                v = T["LZ", c][:, bl * NB:(bl + 1) * NB]
+                nc.scalar.activation(out=v, in_=v, func=ACT.Exp, scale=-1.0)
+
+        def weights():
+            for g in range(G):
+                nc.vector.tensor_copy(
+                    out=w_grp[:, g].rearrange("p (c i) j -> p c j i", i=4),
+                    in_=w_raw[:, g].rearrange("p j (c i) -> p c j i", i=4),
+                )
+            nc.vector.quantize_mx(
+                out=w_codes[:].bitcast(FP8X4), scales=w_scl[:], in_=w_grp[:].rearrange("p g o j -> p (g o j)")
+            )
+
+        def late_pool(c):
+            if c == 0:
+                nc.vector.scalar_tensor_tensor(
+                    out=w_t[:], in0=rs[:], scalar=KAPPA, in1=gam[:], op0=ALU.mult, op1=ALU.mult
+                )
+            LK, LP = T["LK", c], T["LP", c]
+            qv = LK[:].rearrange("p (n b g j c) -> p n g j b c", n=NK, b=CB, g=G, j=J)
+            kv = T["rKs", c][:].rearrange("p (n b g j c) -> p n g j b c", n=NK, b=CB, g=G, j=J)
+            for n in range(NK):
+                for g in range(G):
+                    for j in range(J):
+                        col = (n * G + g) * J + j
+                        nc.vector.scalar_tensor_tensor(
+                            out=qv[:, n, g, j], in0=qv[:, n, g, j], scalar=w_t[:, col:col + 1],
+                            in1=kv[:, n, g, j], op0=ALU.mult, op1=ALU.mult,
+                        )
+            nc.vector.tensor_tensor(out=LP[:], in0=LP[:], in1=T["absP", c][:], op=ALU.mult)
+            nc.vector.tensor_tensor(out=LK[:, 0:NP], in0=LK[:, 0:NP], in1=LK[:, NP:NS], op=ALU.add)
+            nc.vector.tensor_tensor(out=LP[:], in0=LP[:], in1=LK[:, 0:NP], op=ALU.mult)
+
+        def finish(b):
+            c, bl = divmod(b, CB)
+            o_t = outp.tile([P, OT * HW], F32, name="o_t")
+            nc.vector.tensor_tensor(
+                out=o_t[:], in0=T["acc", b][:], in1=T["aJ", c][:, bl * OT * HW:(bl + 1) * OT * HW], op=ALU.mult
+            )
+            nc.gpsimd.dma_start(out=out_v[:, OT * b:OT * (b + 1), :], in_=rows(o_t[:], HW))
+
+        def late_big(b):
+            c, bl = divmod(b, CB)
+            c_b = T["LP", c][:, bl * G * J * CELL:(bl + 1) * G * J * CELL]
+            t_t = one.tile([P, NB], F32, name="t_t")
+            M = G * J * 8
+            nc.vector.tensor_tensor(
+                out=t_t[:].rearrange("p (m ry x2 rx) -> p ry m x2 rx", ry=2, x2=8, rx=2),
+                in0=T["as", c][:, bl * NB:(bl + 1) * NB].rearrange("p (m ry x2 rx) -> p ry m x2 rx", ry=2, x2=8, rx=2),
+                in1=c_b.rearrange("p (m x2) -> p m x2", x2=8).unsqueeze(1).unsqueeze(4).to_broadcast([P, 2, M, 8, 2]),
+                op=ALU.mult,
+            )
+            sc = one.tile([P, G, HW, J], BF16, name="sc", align_bytes=64)
+            tv = t_t[:].rearrange("p (g j c i) -> p g c j i", g=G, j=J, i=4)
+            rv = T["LZ", c][:, bl * NB:(bl + 1) * NB].rearrange("p (g j c i) -> p g c j i", g=G, j=J, i=4)
+            for g in range(G):
+                nc.vector.tensor_tensor(
+                    out=sc[:, g].rearrange("p (c i) j -> p c j i", i=4), in0=tv[:, g], in1=rv[:, g], op=ALU.mult
+                )
+            if b > 0:
+                finish(b - 1)
+            codes = two.tile([P, G * HW], U32, name="codes", align_bytes=64)
+            scl = two.tile([P, G * HW], U8, name="scl", align_bytes=64)
+            nc.vector.quantize_mx(
+                out=codes[:].bitcast(FP8X4), scales=scl[:], in_=sc[:].rearrange("p g w j -> p (g w j)")
+            )
+            T["acc", b] = psum.tile([P, OT * HW], F32, name="acc")
+            for t in range(OT):
+                for g in range(G):
+                    nc.tensor.matmul_mx(
+                        out=T["acc", b][:, t * HW:(t + 1) * HW],
+                        lhsT=w_codes[:, g * 256 + t * P:g * 256 + (t + 1) * P].bitcast(FP8X4),
+                        lhsT_scale=w_scl[:, g * 256 + t * P:g * 256 + (t + 1) * P],
+                        rhs=codes[:, g * HW:(g + 1) * HW].bitcast(FP8X4),
+                        rhs_scale=scl[:, g * HW:(g + 1) * HW],
+                        start=(g == 0), stop=(g == G - 1),
+                    )
+
+        load(0)
+        nc.sync.dma_start(out=rows(vr[:], J), in_=var.rearrange("n (g p j) -> p (n g) j", g=G, p=P, j=J))
+        nc.sync.dma_start(out=rows(gam[:], J), in_=gamma.rearrange("n (g p j) -> p (n g) j", g=G, p=P, j=J))
+        nc.sync.dma_start(out=w_raw[:], in_=W_conv.rearrange("(g p j) o -> p g j o", g=G, p=P, j=J))
+        load(1)
+        s_sign(0)
+        early_a(0)
+        s_ln(0)
+        s_exp(0)
+        weights()
+        early_b(0)
+        for i in range(NCH):
+            if i + 2 < NCH:
+                load(i + 2)
+            if i + 1 < NCH:
+                early_a(i + 1)
+                s_sign(i + 1)
+                s_ln(i + 1)
+                s_exp(i + 1)
+            late_pool(i)
+            for bl in range(CB):
+                late_big(i * CB + bl)
+            if i + 1 < NCH:
+                early_b(i + 1)
+        finish(B - 1)

@@ -73,20 +73,24 @@ def tile_lrpdensenettransition_t_kernel(
         def rows(ap, r):
             return ap.rearrange("p (a r) -> p a r", r=r)
 
-        def load(c):
-            b0 = c * CB
-            sl = slice(G * b0, G * (b0 + CB))
-            for nm, n_cols in (("aK", NS), ("aP", NP), ("z", NZ), ("rK", NS), ("a", NZ)):
+        def load_a(c):
+            sl = slice(G * c * CB, G * (c + 1) * CB)
+            for nm, n_cols in (("aK", NS), ("z", NZ), ("aP", NP)):
+                T[nm, c] = pin.tile([P, n_cols], BF16, name=nm + "_t")
+            for n in range(NK):
+                nc.sync.dma_start(out=rows(T["aK", c][:, n * NP:(n + 1) * NP], J * CELL), in_=aK_v[:, n, sl, :])
+            nc.sync.dma_start(out=rows(T["aP", c][:], J * CELL), in_=aP_v[:, sl, :])
+            nc.sync.dma_start(out=rows(T["z", c][:], J * HW), in_=z_v[:, sl, :])
+
+        def load_b(c):
+            sl = slice(G * c * CB, G * (c + 1) * CB)
+            for nm, n_cols in (("rK", NS), ("a", NZ)):
                 T[nm, c] = pin.tile([P, n_cols], BF16, name=nm + "_t")
             T["aJ", c] = ajp.tile([P, CB * OT * HW], BF16, name="aJ_t")
             for n in range(NK):
-                nc.sync.dma_start(out=rows(T["aK", c][:, n * NP:(n + 1) * NP], J * CELL), in_=aK_v[:, n, sl, :])
-            nc.sync.dma_start(out=rows(T["z", c][:], J * HW), in_=z_v[:, sl, :])
-            nc.sync.dma_start(out=rows(T["aP", c][:], J * CELL), in_=aP_v[:, sl, :])
-            for n in range(NK):
                 nc.sync.dma_start(out=rows(T["rK", c][:, n * NP:(n + 1) * NP], J * CELL), in_=rK_v[:, n, sl, :])
             nc.sync.dma_start(out=rows(T["a", c][:], J * HW), in_=a_v[:, sl, :])
-            nc.sync.dma_start(out=rows(T["aJ", c][:], HW), in_=aJ_v[:, OT * b0:OT * (b0 + CB), :])
+            nc.sync.dma_start(out=rows(T["aJ", c][:], HW), in_=aJ_v[:, OT * c * CB:OT * (c + 1) * CB, :])
 
         def v_abs(dst, src):
             nc.vector.tensor_scalar(
@@ -107,38 +111,42 @@ def tile_lrpdensenettransition_t_kernel(
             T["absZ", c] = one.tile([P, NZ], BF16, name="absZ")
             T["absP", c] = two.tile([P, NP], BF16, name="absP")
             v_abs(T["absK", c], T["aK", c])
-            v_abs(T["absZ", c], T["z", c])
             v_abs(T["absP", c], T["aP", c])
+            v_abs(T["absZ", c], T["z", c])
 
-        def early_b(c):
+        def rks_op(c):
             if not SIGN_K_ON_S:
                 T["sgK", c] = one.tile([P, NS], BF16, name="sgK")
                 v_half_sign(T["sgK", c], T["aK", c])
             T["rKs", c] = one.tile([P, NS], BF16, name="rKs")
             nc.vector.tensor_tensor(out=T["rKs", c][:], in0=T["rK", c][:], in1=T["sgK", c][:], op=ALU.mult)
-            hZ = one.tile([P, NZ], BF16, name="hZ")
-            v_half_sign(hZ, T["z", c])
+
+        def hz_op(c):
+            T["hZ", c] = one.tile([P, NZ], BF16, name="hZ")
+            v_half_sign(T["hZ", c], T["z", c])
+
+        def as_op(c):
             T["as", c] = one.tile([P, NZ], BF16, name="as_t")
-            nc.vector.tensor_tensor(out=T["as", c][:], in0=T["a", c][:], in1=hZ[:], op=ALU.mult)
+            nc.vector.tensor_tensor(out=T["as", c][:], in0=T["a", c][:], in1=T["hZ", c][:], op=ALU.mult)
 
-        def s_ln(c):
-            T["LK", c] = two.tile([P, NS], F32, name="LK")
-            T["LZ", c] = two.tile([P, NZ], F32, name="LZ")
-            T["LP", c] = two.tile([P, NP], F32, name="LP")
-            nc.scalar.activation(out=T["LK", c][:], in_=T["absK", c][:], func=ACT.Ln, bias=E, scale=1.0)
-            nc.scalar.activation(out=T["LZ", c][:], in_=T["absZ", c][:], func=ACT.Ln, bias=E, scale=1.0)
-            nc.scalar.activation(out=T["LP", c][:], in_=T["absP", c][:], func=ACT.Ln, bias=E, scale=1.0)
-            if c == 0:
-                nc.scalar.activation(out=rs[:], in_=vr[:], func=ACT.Ln, bias=BN_EPS, scale=1.0)
+        def s_ln(c, pool_part=True, big_part=True):
+            if pool_part:
+                T["LK", c] = two.tile([P, NS], F32, name="LK")
+                T["LP", c] = two.tile([P, NP], F32, name="LP")
+                nc.scalar.activation(out=T["LK", c][:], in_=T["absK", c][:], func=ACT.Ln, bias=E, scale=1.0)
+                nc.scalar.activation(out=T["LP", c][:], in_=T["absP", c][:], func=ACT.Ln, bias=E, scale=1.0)
+            if big_part:
+                T["LZ", c] = two.tile([P, NZ], F32, name="LZ")
+                nc.scalar.activation(out=T["LZ", c][:], in_=T["absZ", c][:], func=ACT.Ln, bias=E, scale=1.0)
 
-        def s_exp(c):
-            if c == 0:
-                nc.scalar.activation(out=rs[:], in_=rs[:], func=ACT.Exp, scale=-0.5)
-            nc.scalar.activation(out=T["LK", c][:], in_=T["LK", c][:], func=ACT.Exp, scale=-1.0)
-            nc.scalar.activation(out=T["LP", c][:], in_=T["LP", c][:], func=ACT.Exp, scale=-1.0)
-            for bl in range(CB):
-                v = T["LZ", c][:, bl * NB:(bl + 1) * NB]
-                nc.scalar.activation(out=v, in_=v, func=ACT.Exp, scale=-1.0)
+        def s_exp(c, pool_part=True, big_part=True):
+            if pool_part:
+                nc.scalar.activation(out=T["LK", c][:], in_=T["LK", c][:], func=ACT.Exp, scale=-1.0)
+                nc.scalar.activation(out=T["LP", c][:], in_=T["LP", c][:], func=ACT.Exp, scale=-1.0)
+            if big_part:
+                for bl in range(CB):
+                    v = T["LZ", c][:, bl * NB:(bl + 1) * NB]
+                    nc.scalar.activation(out=v, in_=v, func=ACT.Exp, scale=-1.0)
 
         def weights():
             for g in range(G):
@@ -150,13 +158,15 @@ def tile_lrpdensenettransition_t_kernel(
                 out=w_codes[:].bitcast(FP8X4), scales=w_scl[:], in_=w_grp[:].rearrange("p g o j -> p (g o j)")
             )
 
-        def late_pool(c):
+        def g_op(c):
+            nc.vector.tensor_tensor(out=T["LP", c][:], in0=T["LP", c][:], in1=T["absP", c][:], op=ALU.mult)
+
+        def stt_ops(c):
             if c == 0:
                 nc.vector.scalar_tensor_tensor(
                     out=w_t[:], in0=rs[:], scalar=KAPPA, in1=gam[:], op0=ALU.mult, op1=ALU.mult
                 )
-            LK, LP = T["LK", c], T["LP", c]
-            qv = LK[:].rearrange("p (n b g j c) -> p n g j b c", n=NK, b=CB, g=G, j=J)
+            qv = T["LK", c][:].rearrange("p (n b g j c) -> p n g j b c", n=NK, b=CB, g=G, j=J)
             kv = T["rKs", c][:].rearrange("p (n b g j c) -> p n g j b c", n=NK, b=CB, g=G, j=J)
             for n in range(NK):
                 for g in range(G):
@@ -166,9 +176,13 @@ def tile_lrpdensenettransition_t_kernel(
                             out=qv[:, n, g, j], in0=qv[:, n, g, j], scalar=w_t[:, col:col + 1],
                             in1=kv[:, n, g, j], op0=ALU.mult, op1=ALU.mult,
                         )
-            nc.vector.tensor_tensor(out=LP[:], in0=LP[:], in1=T["absP", c][:], op=ALU.mult)
+
+        def sum_op(c):
+            LK = T["LK", c]
             nc.vector.tensor_tensor(out=LK[:, 0:NP], in0=LK[:, 0:NP], in1=LK[:, NP:NS], op=ALU.add)
-            nc.vector.tensor_tensor(out=LP[:], in0=LP[:], in1=LK[:, 0:NP], op=ALU.mult)
+
+        def c_op(c):
+            nc.vector.tensor_tensor(out=T["LP", c][:], in0=T["LP", c][:], in1=T["LK", c][:, 0:NP], op=ALU.mult)
 
         def finish(b):
             c, bl = divmod(b, CB)
@@ -178,30 +192,31 @@ def tile_lrpdensenettransition_t_kernel(
             )
             nc.gpsimd.dma_start(out=out_v[:, OT * b:OT * (b + 1), :], in_=rows(o_t[:], HW))
 
-        def late_big(b):
+        def t_op(b):
             c, bl = divmod(b, CB)
             c_b = T["LP", c][:, bl * G * J * CELL:(bl + 1) * G * J * CELL]
-            t_t = one.tile([P, NB], F32, name="t_t")
-            M = G * J * 8
+            T["t", b] = two.tile([P, NB], F32, name="t_t")
+            T["sc", b] = two.tile([P, G, HW, J], BF16, name="sc", align_bytes=64)
             nc.vector.tensor_tensor(
-                out=t_t[:].rearrange("p (m ry x2 rx) -> p ry m x2 rx", ry=2, x2=8, rx=2),
+                out=T["t", b][:].rearrange("p (m ry x2 rx) -> p ry m x2 rx", ry=2, x2=8, rx=2),
                 in0=T["as", c][:, bl * NB:(bl + 1) * NB].rearrange("p (m ry x2 rx) -> p ry m x2 rx", ry=2, x2=8, rx=2),
-                in1=c_b.rearrange("p (m x2) -> p m x2", x2=8).unsqueeze(1).unsqueeze(4).to_broadcast([P, 2, M, 8, 2]),
+                in1=c_b.rearrange("p (m x2) -> p m x2", x2=8).unsqueeze(1).unsqueeze(4).to_broadcast([P, 2, G * J * 8, 8, 2]),
                 op=ALU.mult,
             )
-            sc = one.tile([P, G, HW, J], BF16, name="sc", align_bytes=64)
-            tv = t_t[:].rearrange("p (g j c i) -> p g c j i", g=G, j=J, i=4)
+
+        def sc_op(b, g):
+            c, bl = divmod(b, CB)
+            tv = T["t", b][:].rearrange("p (g j c i) -> p g c j i", g=G, j=J, i=4)
             rv = T["LZ", c][:, bl * NB:(bl + 1) * NB].rearrange("p (g j c i) -> p g c j i", g=G, j=J, i=4)
-            for g in range(G):
-                nc.vector.tensor_tensor(
-                    out=sc[:, g].rearrange("p (c i) j -> p c j i", i=4), in0=tv[:, g], in1=rv[:, g], op=ALU.mult
-                )
-            if b > 0:
-                finish(b - 1)
+            nc.vector.tensor_tensor(
+                out=T["sc", b][:, g].rearrange("p (c i) j -> p c j i", i=4), in0=tv[:, g], in1=rv[:, g], op=ALU.mult
+            )
+
+        def quant_mm(b):
             codes = two.tile([P, G * HW], U32, name="codes", align_bytes=64)
             scl = two.tile([P, G * HW], U8, name="scl", align_bytes=64)
             nc.vector.quantize_mx(
-                out=codes[:].bitcast(FP8X4), scales=scl[:], in_=sc[:].rearrange("p g w j -> p (g w j)")
+                out=codes[:].bitcast(FP8X4), scales=scl[:], in_=T["sc", b][:].rearrange("p g w j -> p (g w j)")
             )
             T["acc", b] = psum.tile([P, OT * HW], F32, name="acc")
             for t in range(OT):
@@ -215,28 +230,57 @@ def tile_lrpdensenettransition_t_kernel(
                         start=(g == 0), stop=(g == G - 1),
                     )
 
-        load(0)
+        load_a(0)
         nc.sync.dma_start(out=rows(vr[:], J), in_=var.rearrange("n (g p j) -> p (n g) j", g=G, p=P, j=J))
         nc.sync.dma_start(out=rows(gam[:], J), in_=gamma.rearrange("n (g p j) -> p (n g) j", g=G, p=P, j=J))
+        load_b(0)
         nc.sync.dma_start(out=w_raw[:], in_=W_conv.rearrange("(g p j) o -> p g j o", g=G, p=P, j=J))
-        load(1)
+        load_a(1)
+        load_b(1)
         s_sign(0)
         early_a(0)
-        s_ln(0)
-        s_exp(0)
-        weights()
-        early_b(0)
+        s_ln(0, big_part=False)
+        nc.scalar.activation(out=rs[:], in_=vr[:], func=ACT.Ln, bias=BN_EPS, scale=1.0)
+        nc.scalar.activation(out=rs[:], in_=rs[:], func=ACT.Exp, scale=-0.5)
+        s_exp(0, big_part=False)
+        s_ln(0, pool_part=False)
+        s_exp(0, pool_part=False)
+        rks_op(0)
+        hz_op(0)
         for i in range(NCH):
-            if i + 2 < NCH:
-                load(i + 2)
-            if i + 1 < NCH:
+            more = i + 1 < NCH
+            b0 = i * CB
+            stt_ops(i)
+            if more:
                 early_a(i + 1)
                 s_sign(i + 1)
                 s_ln(i + 1)
                 s_exp(i + 1)
-            late_pool(i)
-            for bl in range(CB):
-                late_big(i * CB + bl)
-            if i + 1 < NCH:
-                early_b(i + 1)
+            g_op(i)
+            if i == 0:
+                as_op(0)
+            if i + 2 < NCH:
+                load_a(i + 2)
+                load_b(i + 2)
+            if more:
+                rks_op(i + 1)
+            sum_op(i)
+            if more:
+                hz_op(i + 1)
+            c_op(i)
+            if i == 0:
+                weights()
+            else:
+                finish(b0 - 1)
+            t_op(b0)
+            t_op(b0 + 1)
+            sc_op(b0, 0)
+            sc_op(b0, 1)
+            sc_op(b0 + 1, 0)
+            quant_mm(b0)
+            sc_op(b0 + 1, 1)
+            if more:
+                as_op(i + 1)
+            quant_mm(b0 + 1)
+            finish(b0)
         finish(B - 1)

@@ -190,7 +190,7 @@ def tile_lrpdensenettransition_t_kernel(
             nc.vector.tensor_tensor(
                 out=o_t[:], in0=T["acc", b][:], in1=T["aJ", c][:, bl * OT * HW:(bl + 1) * OT * HW], op=ALU.mult
             )
-            nc.gpsimd.dma_start(out=out_v[:, OT * b:OT * (b + 1), :], in_=rows(o_t[:], HW))
+            nc.sync.dma_start(out=out_v[:, OT * b:OT * (b + 1), :], in_=rows(o_t[:], HW))
 
         def t_op(b):
             c, bl = divmod(b, CB)
@@ -230,6 +230,9 @@ def tile_lrpdensenettransition_t_kernel(
                         start=(g == 0), stop=(g == G - 1),
                     )
 
+        warm = const.tile([P, 1], F32, name="warm")
+        nc.vector.memset(warm[:], 1.0)
+        nc.scalar.activation(out=warm[:], in_=warm[:], func=ACT.Ln)
         load_a(0)
         nc.sync.dma_start(out=rows(vr[:], J), in_=var.rearrange("n (g p j) -> p (n g) j", g=G, p=P, j=J))
         nc.sync.dma_start(out=rows(gam[:], J), in_=gamma.rearrange("n (g p j) -> p (n g) j", g=G, p=P, j=J))

@@ -27,6 +27,7 @@ SIGN_SCALE = 2.0 ** 64
 SIGN_BIAS = 1e-25
 ABS_MASK = 0x7FFF7FFF
 SIGN_K_ON_S = True
+JS = 1
 KAPPA = 0.5 if SIGN_K_ON_S else 1.0
 
 FLOPS = 2 * B * HW * 1024 * 256
@@ -86,10 +87,12 @@ def tile_lrpdensenettransition_t_kernel(
             sl = slice(G * c * CB, G * (c + 1) * CB)
             for nm, n_cols in (("rK", NS), ("a", NZ)):
                 T[nm, c] = pin.tile([P, n_cols], BF16, name=nm + "_t")
-            T["aJ", c] = ajp.tile([P, CB * OT * HW], BF16, name="aJ_t")
             for n in range(NK):
                 nc.sync.dma_start(out=rows(T["rK", c][:, n * NP:(n + 1) * NP], J * CELL), in_=rK_v[:, n, sl, :])
             nc.sync.dma_start(out=rows(T["a", c][:], J * HW), in_=a_v[:, sl, :])
+
+        def load_j(c):
+            T["aJ", c] = ajp.tile([P, CB * OT * HW], BF16, name="aJ_t")
             nc.sync.dma_start(out=rows(T["aJ", c][:], HW), in_=aJ_v[:, OT * c * CB:OT * (c + 1) * CB, :])
 
         def v_abs(dst, src):
@@ -121,9 +124,22 @@ def tile_lrpdensenettransition_t_kernel(
             T["rKs", c] = one.tile([P, NS], BF16, name="rKs")
             nc.vector.tensor_tensor(out=T["rKs", c][:], in0=T["rK", c][:], in1=T["sgK", c][:], op=ALU.mult)
 
+        def by_j(ap):
+            return ap.rearrange("p (a j r) -> p a j r", j=J, r=HW)
+
+        def s_sign_z(c):
+            T["hZ", c] = two.tile([P, NZ], BF16, name="hZ")
+            if JS > 0:
+                nc.scalar.activation(
+                    out=by_j(T["hZ", c][:])[:, :, 0:JS, :], in_=by_j(T["z", c][:])[:, :, 0:JS, :],
+                    func=ACT.Sign, bias=SIGN_BIAS, scale=SIGN_SCALE,
+                )
+
         def hz_op(c):
-            T["hZ", c] = one.tile([P, NZ], BF16, name="hZ")
-            v_half_sign(T["hZ", c], T["z", c])
+            nc.vector.tensor_scalar(
+                out=by_j(T["hZ", c][:])[:, :, JS:J, :], in0=by_j(T["z", c][:])[:, :, JS:J, :],
+                scalar1=0.0, scalar2=0.5, op0=ALU.is_ge, op1=ALU.subtract,
+            )
 
         def as_op(c):
             T["as", c] = one.tile([P, NZ], BF16, name="as_t")
@@ -166,6 +182,9 @@ def tile_lrpdensenettransition_t_kernel(
                 nc.vector.scalar_tensor_tensor(
                     out=w_t[:], in0=rs[:], scalar=KAPPA, in1=gam[:], op0=ALU.mult, op1=ALU.mult
                 )
+                if JS > 0:
+                    wj = rows(w_t[:], J)[:, :, 0:JS]
+                    nc.vector.tensor_scalar(out=wj, in0=wj, scalar1=0.5, scalar2=None, op0=ALU.mult)
             qv = T["LK", c][:].rearrange("p (n b g j c) -> p n g j b c", n=NK, b=CB, g=G, j=J)
             kv = T["rKs", c][:].rearrange("p (n b g j c) -> p n g j b c", n=NK, b=CB, g=G, j=J)
             for n in range(NK):
@@ -239,17 +258,22 @@ def tile_lrpdensenettransition_t_kernel(
         load_b(0)
         nc.sync.dma_start(out=w_raw[:], in_=W_conv.rearrange("(g p j) o -> p g j o", g=G, p=P, j=J))
         load_a(1)
+        load_j(0)
         load_b(1)
+        load_j(1)
         s_sign(0)
         early_a(0)
         s_ln(0, big_part=False)
         nc.scalar.activation(out=rs[:], in_=vr[:], func=ACT.Ln, bias=BN_EPS, scale=1.0)
         nc.scalar.activation(out=rs[:], in_=rs[:], func=ACT.Exp, scale=-0.5)
         s_exp(0, big_part=False)
+        s_sign_z(0)
         s_ln(0, pool_part=False)
         s_exp(0, pool_part=False)
         rks_op(0)
         hz_op(0)
+        as_op(0)
+        weights()
         for i in range(NCH):
             more = i + 1 < NCH
             b0 = i * CB
@@ -257,23 +281,21 @@ def tile_lrpdensenettransition_t_kernel(
             if more:
                 early_a(i + 1)
                 s_sign(i + 1)
+                s_sign_z(i + 1)
                 s_ln(i + 1)
                 s_exp(i + 1)
             g_op(i)
-            if i == 0:
-                as_op(0)
             if i + 2 < NCH:
                 load_a(i + 2)
                 load_b(i + 2)
+                load_j(i + 2)
             if more:
                 rks_op(i + 1)
             sum_op(i)
             if more:
                 hz_op(i + 1)
             c_op(i)
-            if i == 0:
-                weights()
-            else:
+            if i > 0:
                 finish(b0 - 1)
             t_op(b0)
             t_op(b0 + 1)

@@ -74,26 +74,27 @@ def tile_lrpdensenettransition_t_kernel(
         def rows(ap, r):
             return ap.rearrange("p (a r) -> p a r", r=r)
 
-        def load_a(c):
-            sl = slice(G * c * CB, G * (c + 1) * CB)
-            for nm, n_cols in (("aK", NS), ("z", NZ), ("aP", NP)):
-                T[nm, c] = pin.tile([P, n_cols], BF16, name=nm + "_t")
-            for n in range(NK):
-                nc.sync.dma_start(out=rows(T["aK", c][:, n * NP:(n + 1) * NP], J * CELL), in_=aK_v[:, n, sl, :])
-            nc.sync.dma_start(out=rows(T["aP", c][:], J * CELL), in_=aP_v[:, sl, :])
-            nc.sync.dma_start(out=rows(T["z", c][:], J * HW), in_=z_v[:, sl, :])
+        WIDTH = {"aK": NS, "rK": NS, "aP": NP, "z": NZ, "a": NZ}
+        VIEW = {"aP": aP_v, "z": z_v, "a": a_v}
+        STACK = {"aK": aK_v, "rK": rK_v}
 
-        def load_b(c):
+        def ld(nm, c):
             sl = slice(G * c * CB, G * (c + 1) * CB)
-            for nm, n_cols in (("rK", NS), ("a", NZ)):
-                T[nm, c] = pin.tile([P, n_cols], BF16, name=nm + "_t")
-            for n in range(NK):
-                nc.sync.dma_start(out=rows(T["rK", c][:, n * NP:(n + 1) * NP], J * CELL), in_=rK_v[:, n, sl, :])
-            nc.sync.dma_start(out=rows(T["a", c][:], J * HW), in_=a_v[:, sl, :])
+            T[nm, c] = pin.tile([P, WIDTH[nm]], BF16, name=nm + "_t")
+            if nm in STACK:
+                for n in range(NK):
+                    nc.sync.dma_start(out=rows(T[nm, c][:, n * NP:(n + 1) * NP], J * CELL), in_=STACK[nm][:, n, sl, :])
+            else:
+                nc.sync.dma_start(out=rows(T[nm, c][:], WIDTH[nm] // (G * CB)), in_=VIEW[nm][:, sl, :])
 
         def load_j(c):
             T["aJ", c] = ajp.tile([P, CB * OT * HW], BF16, name="aJ_t")
             nc.sync.dma_start(out=rows(T["aJ", c][:], HW), in_=aJ_v[:, OT * c * CB:OT * (c + 1) * CB, :])
+
+        def load(c):
+            for nm in ("aK", "aP", "z", "rK", "a"):
+                ld(nm, c)
+            load_j(c)
 
         def v_abs(dst, src):
             nc.vector.tensor_scalar(
@@ -109,12 +110,14 @@ def tile_lrpdensenettransition_t_kernel(
                 T["sgK", c] = one.tile([P, NS], BF16, name="sgK")
                 nc.scalar.activation(out=T["sgK", c][:], in_=T["aK", c][:], func=ACT.Sign, bias=SIGN_BIAS, scale=SIGN_SCALE)
 
-        def early_a(c):
+        def abs_pool(c):
             T["absK", c] = one.tile([P, NS], BF16, name="absK")
-            T["absZ", c] = one.tile([P, NZ], BF16, name="absZ")
             T["absP", c] = two.tile([P, NP], BF16, name="absP")
             v_abs(T["absK", c], T["aK", c])
             v_abs(T["absP", c], T["aP", c])
+
+        def abs_big(c):
+            T["absZ", c] = one.tile([P, NZ], BF16, name="absZ")
             v_abs(T["absZ", c], T["z", c])
 
         def rks_op(c):
@@ -252,43 +255,44 @@ def tile_lrpdensenettransition_t_kernel(
         warm = const.tile([P, 1], F32, name="warm")
         nc.vector.memset(warm[:], 1.0)
         nc.scalar.activation(out=warm[:], in_=warm[:], func=ACT.Ln)
-        load_a(0)
+        ld("aK", 0)
+        ld("aP", 0)
         nc.sync.dma_start(out=rows(vr[:], J), in_=var.rearrange("n (g p j) -> p (n g) j", g=G, p=P, j=J))
         nc.sync.dma_start(out=rows(gam[:], J), in_=gamma.rearrange("n (g p j) -> p (n g) j", g=G, p=P, j=J))
-        load_b(0)
+        ld("rK", 0)
         nc.sync.dma_start(out=w_raw[:], in_=W_conv.rearrange("(g p j) o -> p g j o", g=G, p=P, j=J))
-        load_a(1)
+        ld("z", 0)
+        ld("a", 0)
         load_j(0)
-        load_b(1)
-        load_j(1)
+        load(1)
         s_sign(0)
-        early_a(0)
+        abs_pool(0)
         s_ln(0, big_part=False)
         nc.scalar.activation(out=rs[:], in_=vr[:], func=ACT.Ln, bias=BN_EPS, scale=1.0)
         nc.scalar.activation(out=rs[:], in_=rs[:], func=ACT.Exp, scale=-0.5)
         s_exp(0, big_part=False)
+        rks_op(0)
+        weights()
+        abs_big(0)
         s_sign_z(0)
         s_ln(0, pool_part=False)
         s_exp(0, pool_part=False)
-        rks_op(0)
         hz_op(0)
         as_op(0)
-        weights()
         for i in range(NCH):
             more = i + 1 < NCH
             b0 = i * CB
             stt_ops(i)
             if more:
-                early_a(i + 1)
+                abs_pool(i + 1)
+                abs_big(i + 1)
                 s_sign(i + 1)
                 s_sign_z(i + 1)
                 s_ln(i + 1)
                 s_exp(i + 1)
             g_op(i)
             if i + 2 < NCH:
-                load_a(i + 2)
-                load_b(i + 2)
-                load_j(i + 2)
+                load(i + 2)
             if more:
                 rks_op(i + 1)
             sum_op(i)

@@ -293,8 +293,6 @@ def tile_lrpdensenettransition_t_kernel(
             g_op(i)
             if i + 2 < NCH:
                 load(i + 2)
-            if more:
-                rks_op(i + 1)
             sum_op(i)
             if more:
                 hz_op(i + 1)
@@ -305,6 +303,8 @@ def tile_lrpdensenettransition_t_kernel(
             t_op(b0 + 1)
             sc_op(b0, 0)
             sc_op(b0, 1)
+            if more:
+                rks_op(i + 1)
             sc_op(b0 + 1, 0)
             quant_mm(b0)
             sc_op(b0 + 1, 1)

from contextlib import ExitStack

import concourse.mybir as mybir

FP8X4 = mybir.dt.float8_e4m3fn_x4
BF16 = mybir.dt.bfloat16
F32 = mybir.dt.float32
I32 = mybir.dt.int32
U32 = mybir.dt.uint32
U8 = mybir.dt.uint8
ALU = mybir.AluOpType
ACT = mybir.ActivationFunctionType

P = 128
NK = 2
B = 16
G = 2
J = 4
HW = 256
CELL = 64
OT = 2
CB = 2
NCH = B // CB
E = 0.01
BN_EPS = 1e-5
SIGN_SCALE = 2.0 ** 64
SIGN_BIAS = 1e-25
ABS_MASK = 0x7FFF7FFF
SIGN_K_ON_S = True
JS = 1
KAPPA = 0.5 if SIGN_K_ON_S else 1.0

FLOPS = 2 * B * HW * 1024 * 256


def tile_lrpdensenettransition_t_kernel(
    tc, rK_stack, aK_stack, gamma, var, aKPool, aJ_pool, aK_conv, aJ_conv, W_conv, out
):
    nc = tc.nc
    NP = CB * G * J * CELL
    NS = NK * NP
    NB = G * J * HW
    NZ = CB * NB
    NW = NK * G * J

    rK_v = rK_stack.rearrange("n b (g p j) h w -> p n (b g) (j h w)", g=G, p=P, j=J)
    aK_v = aK_stack.rearrange("n b (g p j) h w -> p n (b g) (j h w)", g=G, p=P, j=J)
    aP_v = aKPool.rearrange("b (g p j) h w -> p (b g) (j h w)", g=G, p=P, j=J)
    a_v = aJ_pool.rearrange("b (g p j) h w -> p (b g) (j h w)", g=G, p=P, j=J)
    z_v = aK_conv.rearrange("b (g p j) h w -> p (b g) (j h w)", g=G, p=P, j=J)
    aJ_v = aJ_conv.rearrange("b (t p) h w -> p (b t) (h w)", t=OT, p=P)
    out_v = out.rearrange("b (t p) h w -> p (b t) (h w)", t=OT, p=P)

    with ExitStack() as ctx:
        const = ctx.enter_context(tc.tile_pool(name="const", bufs=1))
        pin = ctx.enter_context(tc.tile_pool(name="pin", bufs=2))
        one = ctx.enter_context(tc.tile_pool(name="one", bufs=1))
        two = ctx.enter_context(tc.tile_pool(name="two", bufs=2))
        ajp = ctx.enter_context(tc.tile_pool(name="ajp", bufs=4))
        outp = ctx.enter_context(tc.tile_pool(name="outp", bufs=3))
        psum = ctx.enter_context(tc.psum_pool(name="psum", bufs=2))
        ctx.enter_context(tc.manual_schedule())

        gam = const.tile([P, NW], BF16, name="gam")
        vr = const.tile([P, NW], BF16, name="vr")
        rs = const.tile([P, NW], F32, name="rs")
        w_t = const.tile([P, NW], F32, name="w_t")
        w_raw = const.tile([P, G, J, 256], BF16, name="w_raw")
        w_grp = const.tile([P, G, 256, J], BF16, name="w_grp", align_bytes=64)
        w_codes = const.tile([P, G * 256], U32, name="w_codes", align_bytes=64)
        w_scl = const.tile([P, G * 256], U8, name="w_scl", align_bytes=64)
        T = {}

        def rows(ap, r):
            return ap.rearrange("p (a r) -> p a r", r=r)

        WIDTH = {"aK": NS, "rK": NS, "aP": NP, "z": NZ, "a": NZ}
        VIEW = {"aP": aP_v, "z": z_v, "a": a_v}
        STACK = {"aK": aK_v, "rK": rK_v}

        def ld(nm, c):
            sl = slice(G * c * CB, G * (c + 1) * CB)
            T[nm, c] = pin.tile([P, WIDTH[nm]], BF16, name=nm + "_t")
            if nm in STACK:
                for n in range(NK):
                    nc.sync.dma_start(out=rows(T[nm, c][:, n * NP:(n + 1) * NP], J * CELL), in_=STACK[nm][:, n, sl, :])
            else:
                nc.sync.dma_start(out=rows(T[nm, c][:], WIDTH[nm] // (G * CB)), in_=VIEW[nm][:, sl, :])

        def load_j(c):
            T["aJ", c] = ajp.tile([P, CB * OT * HW], BF16, name="aJ_t")
            nc.sync.dma_start(out=rows(T["aJ", c][:], HW), in_=aJ_v[:, OT * c * CB:OT * (c + 1) * CB, :])

        def load(c):
            for nm in ("aK", "aP", "z", "rK", "a"):
                ld(nm, c)
            load_j(c)

        def v_abs(dst, src):
            nc.vector.tensor_scalar(
                out=dst[:].bitcast(I32), in0=src[:].bitcast(I32),
                scalar1=ABS_MASK, scalar2=None, op0=ALU.bitwise_and,
            )

        def v_half_sign(dst, src):
            nc.vector.tensor_scalar(out=dst[:], in0=src[:], scalar1=0.0, scalar2=0.5, op0=ALU.is_ge, op1=ALU.subtract)

        def s_sign(c):
            if SIGN_K_ON_S:
                T["sgK", c] = one.tile([P, NS], BF16, name="sgK")
                nc.scalar.activation(out=T["sgK", c][:], in_=T["aK", c][:], func=ACT.Sign, bias=SIGN_BIAS, scale=SIGN_SCALE)

        def abs_pool(c):
            T["absK", c] = one.tile([P, NS], BF16, name="absK")
            T["absP", c] = two.tile([P, NP], BF16, name="absP")
            v_abs(T["absK", c], T["aK", c])
            v_abs(T["absP", c], T["aP", c])

        def abs_big(c):
            T["absZ", c] = one.tile([P, NZ], BF16, name="absZ")
            v_abs(T["absZ", c], T["z", c])

        def rks_op(c):
            if not SIGN_K_ON_S:
                T["sgK", c] = one.tile([P, NS], BF16, name="sgK")
                v_half_sign(T["sgK", c], T["aK", c])
            T["rKs", c] = one.tile([P, NS], BF16, name="rKs")
            nc.vector.tensor_tensor(out=T["rKs", c][:], in0=T["rK", c][:], in1=T["sgK", c][:], op=ALU.mult)

        def by_j(ap):
            return ap.rearrange("p (a j r) -> p a j r", j=J, r=HW)

        def s_sign_z(c):
            T["hZ", c] = two.tile([P, NZ], BF16, name="hZ")
            if JS > 0:
                nc.scalar.activation(
                    out=by_j(T["hZ", c][:])[:, :, 0:JS, :], in_=by_j(T["z", c][:])[:, :, 0:JS, :],
                    func=ACT.Sign, bias=SIGN_BIAS, scale=SIGN_SCALE,
                )

        def hz_op(c):
            nc.vector.tensor_scalar(
                out=by_j(T["hZ", c][:])[:, :, JS:J, :], in0=by_j(T["z", c][:])[:, :, JS:J, :],
                scalar1=0.0, scalar2=0.5, op0=ALU.is_ge, op1=ALU.subtract,
            )

        def as_op(c):
            T["as", c] = one.tile([P, NZ], BF16, name="as_t")
            nc.vector.tensor_tensor(out=T["as", c][:], in0=T["a", c][:], in1=T["hZ", c][:], op=ALU.mult)

        def s_ln(c, pool_part=True, big_part=True):
            if pool_part:
                T["LK", c] = two.tile([P, NS], F32, name="LK")
                T["LP", c] = two.tile([P, NP], F32, name="LP")
                nc.scalar.activation(out=T["LK", c][:], in_=T["absK", c][:], func=ACT.Ln, bias=E, scale=1.0)
                nc.scalar.activation(out=T["LP", c][:], in_=T["absP", c][:], func=ACT.Ln, bias=E, scale=1.0)
            if big_part:
                T["LZ", c] = two.tile([P, NZ], F32, name="LZ")
                nc.scalar.activation(out=T["LZ", c][:], in_=T["absZ", c][:], func=ACT.Ln, bias=E, scale=1.0)

        def s_exp(c, pool_part=True, big_part=True):
            if pool_part:
                nc.scalar.activation(out=T["LK", c][:], in_=T["LK", c][:], func=ACT.Exp, scale=-1.0)
                nc.scalar.activation(out=T["LP", c][:], in_=T["LP", c][:], func=ACT.Exp, scale=-1.0)
            if big_part:
                for bl in range(CB):
                    v = T["LZ", c][:, bl * NB:(bl + 1) * NB]
                    nc.scalar.activation(out=v, in_=v, func=ACT.Exp, scale=-1.0)

        def weights():
            for g in range(G):
                nc.vector.tensor_copy(
                    out=w_grp[:, g].rearrange("p (c i) j -> p c j i", i=4),
                    in_=w_raw[:, g].rearrange("p j (c i) -> p c j i", i=4),
                )
            nc.vector.quantize_mx(
                out=w_codes[:].bitcast(FP8X4), scales=w_scl[:], in_=w_grp[:].rearrange("p g o j -> p (g o j)")
            )

        def g_op(c):
            nc.vector.tensor_tensor(out=T["LP", c][:], in0=T["LP", c][:], in1=T["absP", c][:], op=ALU.mult)

        def stt_ops(c):
            if c == 0:
                nc.vector.scalar_tensor_tensor(
                    out=w_t[:], in0=rs[:], scalar=KAPPA, in1=gam[:], op0=ALU.mult, op1=ALU.mult
                )
                if JS > 0:
                    wj = rows(w_t[:], J)[:, :, 0:JS]
                    nc.vector.tensor_scalar(out=wj, in0=wj, scalar1=0.5, scalar2=None, op0=ALU.mult)
            qv = T["LK", c][:].rearrange("p (n b g j c) -> p n g j b c", n=NK, b=CB, g=G, j=J)
            kv = T["rKs", c][:].rearrange("p (n b g j c) -> p n g j b c", n=NK, b=CB, g=G, j=J)
            for n in range(NK):
                for g in range(G):
                    for j in range(J):
                        col = (n * G + g) * J + j
                        nc.vector.scalar_tensor_tensor(
                            out=qv[:, n, g, j], in0=qv[:, n, g, j], scalar=w_t[:, col:col + 1],
                            in1=kv[:, n, g, j], op0=ALU.mult, op1=ALU.mult,
                        )

        def sum_op(c):
            LK = T["LK", c]
            nc.vector.tensor_tensor(out=LK[:, 0:NP], in0=LK[:, 0:NP], in1=LK[:, NP:NS], op=ALU.add)

        def c_op(c):
            nc.vector.tensor_tensor(out=T["LP", c][:], in0=T["LP", c][:], in1=T["LK", c][:, 0:NP], op=ALU.mult)

        def finish(b):
            c, bl = divmod(b, CB)
            o_t = outp.tile([P, OT * HW], F32, name="o_t")
            nc.vector.tensor_tensor(
                out=o_t[:], in0=T["acc", b][:], in1=T["aJ", c][:, bl * OT * HW:(bl + 1) * OT * HW], op=ALU.mult
            )
            nc.sync.dma_start(out=out_v[:, OT * b:OT * (b + 1), :], in_=rows(o_t[:], HW))

        def t_op(b):
            c, bl = divmod(b, CB)
            c_b = T["LP", c][:, bl * G * J * CELL:(bl + 1) * G * J * CELL]
            T["t", b] = two.tile([P, NB], F32, name="t_t")
            T["sc", b] = two.tile([P, G, HW, J], BF16, name="sc", align_bytes=64)
            nc.vector.tensor_tensor(
                out=T["t", b][:].rearrange("p (m ry x2 rx) -> p ry m x2 rx", ry=2, x2=8, rx=2),
                in0=T["as", c][:, bl * NB:(bl + 1) * NB].rearrange("p (m ry x2 rx) -> p ry m x2 rx", ry=2, x2=8, rx=2),
                in1=c_b.rearrange("p (m x2) -> p m x2", x2=8).unsqueeze(1).unsqueeze(4).to_broadcast([P, 2, G * J * 8, 8, 2]),
                op=ALU.mult,
            )

        def sc_op(b, g):
            c, bl = divmod(b, CB)
            tv = T["t", b][:].rearrange("p (g j c i) -> p g c j i", g=G, j=J, i=4)
            rv = T["LZ", c][:, bl * NB:(bl + 1) * NB].rearrange("p (g j c i) -> p g c j i", g=G, j=J, i=4)
            nc.vector.tensor_tensor(
                out=T["sc", b][:, g].rearrange("p (c i) j -> p c j i", i=4), in0=tv[:, g], in1=rv[:, g], op=ALU.mult
            )

        def quant_mm(b):
            codes = two.tile([P, G * HW], U32, name="codes", align_bytes=64)
            scl = two.tile([P, G * HW], U8, name="scl", align_bytes=64)
            nc.vector.quantize_mx(
                out=codes[:].bitcast(FP8X4), scales=scl[:], in_=T["sc", b][:].rearrange("p g w j -> p (g w j)")
            )
            T["acc", b] = psum.tile([P, OT * HW], F32, name="acc")
            for t in range(OT):
                for g in range(G):
                    nc.tensor.matmul_mx(
                        out=T["acc", b][:, t * HW:(t + 1) * HW],
                        lhsT=w_codes[:, g * 256 + t * P:g * 256 + (t + 1) * P].bitcast(FP8X4),
                        lhsT_scale=w_scl[:, g * 256 + t * P:g * 256 + (t + 1) * P],
                        rhs=codes[:, g * HW:(g + 1) * HW].bitcast(FP8X4),
                        rhs_scale=scl[:, g * HW:(g + 1) * HW],
                        start=(g == 0), stop=(g == G - 1),
                    )

        warm = const.tile([P, 1], F32, name="warm")
        nc.vector.memset(warm[:], 1.0)
        nc.scalar.activation(out=warm[:], in_=warm[:], func=ACT.Ln)
        ld("aK", 0)
        ld("aP", 0)
        nc.sync.dma_start(out=rows(vr[:], J), in_=var.rearrange("n (g p j) -> p (n g) j", g=G, p=P, j=J))
        nc.sync.dma_start(out=rows(gam[:], J), in_=gamma.rearrange("n (g p j) -> p (n g) j", g=G, p=P, j=J))
        ld("rK", 0)
        nc.sync.dma_start(out=w_raw[:], in_=W_conv.rearrange("(g p j) o -> p g j o", g=G, p=P, j=J))
        ld("z", 0)
        ld("a", 0)
        load_j(0)
        load(1)
        s_sign(0)
        abs_pool(0)
        s_ln(0, big_part=False)
        nc.scalar.activation(out=rs[:], in_=vr[:], func=ACT.Ln, bias=BN_EPS, scale=1.0)
        nc.scalar.activation(out=rs[:], in_=rs[:], func=ACT.Exp, scale=-0.5)
        s_exp(0, big_part=False)
        rks_op(0)
        weights()
        abs_big(0)
        s_sign_z(0)
        s_ln(0, pool_part=False)
        s_exp(0, pool_part=False)
        hz_op(0)
        as_op(0)
        for i in range(NCH):
            more = i + 1 < NCH
            b0 = i * CB
            stt_ops(i)
            if more:
                abs_pool(i + 1)
                abs_big(i + 1)
                s_sign(i + 1)
                s_sign_z(i + 1)
                s_ln(i + 1)
                s_exp(i + 1)
            g_op(i)
            if i + 2 < NCH:
                load(i + 2)
            sum_op(i)
            if more:
                hz_op(i + 1)
            c_op(i)
            if i > 0:
                finish(b0 - 1)
            t_op(b0)
            t_op(b0 + 1)
            sc_op(b0, 0)
            sc_op(b0, 1)
            if more:
                rks_op(i + 1)
            sc_op(b0 + 1, 0)
            quant_mm(b0)
            sc_op(b0 + 1, 1)
            if more:
                as_op(i + 1)
            quant_mm(b0 + 1)
            finish(b0)
        finish(B - 1)
